import numpy as np
import ml_dtypes


def mxq(x, axis, fmt="e4m3"):
    dtype, down = {"e4m3": (ml_dtypes.float8_e4m3fn, 7), "e5m2": (ml_dtypes.float8_e5m2, 14)}[fmt]
    v = np.moveaxis(np.asarray(x, np.float32).astype(ml_dtypes.bfloat16).astype(np.float64), axis, -1)
    blocks = v.reshape(v.shape[:-1] + (-1, 32))
    amax = np.abs(blocks).max(-1, keepdims=True)
    byte = np.maximum(np.where(amax > 0, np.frexp(amax)[1] - 1 + 127, 0) - down, 1)
    scale = np.exp2(byte - 127.0)
    codes = (blocks / scale).astype(np.float32).astype(dtype).astype(np.float64)
    return np.moveaxis((codes * scale).reshape(v.shape), -1, axis)


WIDE = False


def mx_kscale(k):
    if not WIDE:
        return np.ones(k)
    levels = np.array([10, -10, 5, -5, 0])
    a = np.random.permutation(np.resize(levels, k // 512 * 4)).reshape(k // 512, 4)
    idx = np.arange(k)
    return np.exp2(a[idx // 512, idx % 128 // 32])


BF16 = ml_dtypes.bfloat16


def bf(x):
    return np.asarray(x, np.float32).astype(BF16)


def f64(x):
    return np.asarray(x).astype(np.float64)


N, C_IN, H, W, C_OUT, K, POOL = 4, 8192, 16, 16, 128, 3, 2
SUBTRACT_VALUE = 0.5
NEG_INIT = -1000000000.0
PAD = K // 2
HP, WP = H // POOL, W // POOL


def setup_inputs():
    s = mx_kscale(C_IN)[None, :, None, None]
    x = (np.random.standard_normal((N, C_IN, H, W)) + 0.5) * s
    weight = (np.random.standard_normal((C_OUT, C_IN, K, K)) * 1.8 / np.sqrt(C_IN) - 4.0 / C_IN) / s
    bias = 2.0 + 0.5 * np.random.standard_normal(C_OUT)
    return {"x": bf(x), "weight": bf(weight), "bias": bf(bias)}


def reference(x, weight, bias):
    xq = mxq(f64(x), 1, "e4m3")
    wq = mxq(f64(weight), 1, "e4m3")
    b = f64(bias)
    max_val = np.full((N, C_OUT, HP, WP), NEG_INIT)
    for kh in range(K):
        for kw in range(K):
            sh, rh = (kh - PAD) // POOL, (kh - PAD) % POOL
            sw, rw = (kw - PAD) // POOL, (kw - PAD) % POOL
            xs = xq[:, :, rh::POOL, rw::POOL]
            t = (wq[:, :, kh, kw] @ xs.reshape(N, C_IN, HP * WP)).reshape(N, C_OUT, HP, WP)
            t = t + b[None, :, None, None] - SUBTRACT_VALUE
            hs = t * np.clip(t + 3.0, 0.0, 6.0) / 6.0
            p0, p1 = max(0, -sh), min(HP, HP - sh)
            q0, q1 = max(0, -sw), min(WP, WP - sw)
            max_val[:, :, p0:p1, q0:q1] = np.maximum(max_val[:, :, p0:p1, q0:q1], hs[:, :, p0 + sh:p1 + sh, q0 + sw:q1 + sw])
    return max_val * np.tanh(np.log(1.0 + np.exp(max_val)))

@@ -1,0 +1,216 @@
+from contextlib import ExitStack
+
+import concourse.mybir as mybir
+from concourse.masks import make_identity
+
+BF16 = mybir.dt.bfloat16
+F32 = mybir.dt.float32
+U32 = mybir.dt.uint32
+U8 = mybir.dt.uint8
+FP8X4 = mybir.dt.float8_e4m3fn_x4
+ACT = mybir.ActivationFunctionType
+ALU = mybir.AluOpType
+
+P = 128
+PACK = 4
+K_PASS = P * PACK
+IMAGES, C_IN, HEIGHT, WIDTH = 4, 8192, 16, 16
+C_OUT, KERNEL = 128, 3
+TAPS = KERNEL * KERNEL
+PASSES = C_IN // K_PASS
+OUT_H, OUT_W = HEIGHT // 2, WIDTH // 2
+COLS = IMAGES * OUT_H * OUT_W
+CLASSES = 4
+W_COLS = TAPS * C_OUT
+CENTER = 4
+
+FLOPS = 2 * TAPS * C_OUT * C_IN * COLS
+
+RAW_BUFS = 7
+GRP_BUFS = 3
+VECTOR_TAPS = 7
+REGIONS = 4
+
+
+def tap_class(tap):
+    kh, kw = divmod(tap, KERNEL)
+    return 2 * ((kh - 1) % 2) + (kw - 1) % 2
+
+
+def tile_modelnew_pa_k_kernel(tc, x, weight, bias, out):
+    nc = tc.nc
+    with ExitStack() as stack:
+        keep = stack.enter_context(tc.tile_pool(name="keep", bufs=1))
+        raw_pool = stack.enter_context(tc.tile_pool(name="raw", bufs=RAW_BUFS))
+        grp_pool = stack.enter_context(tc.tile_pool(name="grp", bufs=GRP_BUFS))
+
+        ident = keep.tile([P, P], F32)
+        make_identity(nc, ident[:])
+
+        zero = keep.tile([P, 1], F32)
+        one = keep.tile([P, 1], F32)
+        nc.vector.memset(zero[:], 0.0)
+        nc.scalar.activation(out=one[:], in_=zero[:], func=ACT.Exp)
+
+        bias_bf = keep.tile([P, 1], BF16)
+        with nc.allow_non_contiguous_dma(reason="128 bias values, one to a partition"):
+            nc.sync.dma_start(out=bias_bf[:], in_=bias.rearrange("(o one) -> o one", one=1))
+        shift_t = keep.tile([P, 1], F32)
+        shift_r = keep.tile([P, 1], F32)
+        nc.vector.tensor_scalar_add(out=shift_t[:], in0=bias_bf[:], scalar1=-0.5)
+        nc.vector.tensor_scalar_add(out=shift_r[:], in0=bias_bf[:], scalar1=2.5)
+
+        w_codes = keep.tile([P, PASSES * W_COLS], U32, align_bytes=64)
+        w_scales = keep.tile([P, PASSES * W_COLS], U8, align_bytes=64)
+        c_codes = keep.tile([P, PASSES * COLS], U32, align_bytes=64)
+        c_scales = keep.tile([P, PASSES * COLS], U8, align_bytes=64)
+
+        w_rows = weight.rearrange("o c kh kw -> o (c kh kw)")
+        with tc.tile_pool(name="sorted", bufs=2) as sorted_pool, tc.psum_pool(name="turned", bufs=8) as turned_pool:
+            for g in range(PASSES):
+                w_raw = raw_pool.tile([P, K_PASS * TAPS], BF16, tag="raw")
+                nc.sync.dma_start(out=w_raw[:], in_=w_rows[:, g * K_PASS * TAPS : (g + 1) * K_PASS * TAPS])
+
+                w_sorted = sorted_pool.tile([P, K_PASS * TAPS], BF16)
+                src = w_raw[:].rearrange("o (p half e t) -> o half p e t", half=2, e=2, t=TAPS)
+                dst = w_sorted[:].rearrange("o (t half p e) -> o half p e t", half=2, e=2, t=TAPS)
+                for half in range(2):
+                    for t0 in range(0, VECTOR_TAPS, REGIONS):
+                        t1 = min(t0 + REGIONS, VECTOR_TAPS)
+                        nc.vector.tensor_copy(out=dst[:, half, :, :, t0:t1], in_=src[:, half, :, :, t0:t1])
+                    nc.scalar.copy(out=dst[:, half, :, :, VECTOR_TAPS:TAPS], in_=src[:, half, :, :, VECTOR_TAPS:TAPS])
+
+                words = w_sorted[:].bitcast(F32)
+                w_grouped = grp_pool.tile([P, K_PASS * TAPS], BF16, tag="grp", align_bytes=64)
+                grouped_words = w_grouped[:].bitcast(F32)
+                for t0 in range(0, TAPS, 2):
+                    n_taps = min(2, TAPS - t0)
+                    turned = turned_pool.tile([P, 2 * 2 * P], F32)
+                    for k in range(2 * n_taps):
+                        nc.tensor.transpose(
+                            turned[:, k * P : (k + 1) * P],
+                            words[:, (2 * t0 + k) * P : (2 * t0 + k + 1) * P],
+                            ident[:],
+                        )
+                    nc.scalar.copy(
+                        out=grouped_words[:, 2 * t0 * P : 2 * (t0 + n_taps) * P].rearrange(
+                            "p (t o half) -> p t o half", o=P, half=2
+                        ),
+                        in_=turned[:, 0 : 2 * n_taps * P].rearrange("p (t half o) -> p t o half", o=P, half=2),
+                    )
+
+                for c0, c1 in ((0, 1024), (1024, W_COLS)):
+                    nc.vector.quantize_mx(
+                        out=w_codes[:, g * W_COLS + c0 : g * W_COLS + c1].bitcast(FP8X4),
+                        scales=w_scales[:, g * W_COLS + c0 : g * W_COLS + c1],
+                        in_=w_grouped[:, PACK * c0 : PACK * c1],
+                    )
+
+        xq_pool = stack.enter_context(tc.tile_pool(name="xq", bufs=3))
+        post = stack.enter_context(tc.tile_pool(name="post", bufs=2))
+        acc_pool = stack.enter_context(tc.psum_pool(name="acc", bufs=8))
+
+        def multiply(acc, tap, g, codes, scales):
+            nc.tensor.matmul_mx(
+                out=acc[:],
+                lhsT=w_codes[:, g * W_COLS + tap * C_OUT : g * W_COLS + (tap + 1) * C_OUT].bitcast(FP8X4),
+                lhsT_scale=w_scales[:, g * W_COLS + tap * C_OUT : g * W_COLS + (tap + 1) * C_OUT],
+                rhs=codes.bitcast(FP8X4),
+                rhs_scale=scales,
+                start=(g == 0),
+                stop=(g == PASSES - 1),
+            )
+
+        stream_taps = [tap for tap in reversed(range(TAPS)) if tap != CENTER]
+        sums = {}
+        for tap in stream_taps:
+            sums[tap] = acc_pool.tile([P, COLS], F32, name="acc%d" % tap, tag="acc")
+
+        for g in range(PASSES):
+            x_raw = raw_pool.tile([P, K_PASS * TAPS], BF16, tag="raw")
+            nc.sync.dma_start(
+                out=x_raw[:, 0 : PACK * CLASSES * COLS].rearrange("p (n q) -> p n q", n=IMAGES),
+                in_=x[:, g * K_PASS : (g + 1) * K_PASS, :, :].rearrange("n (p t) h w -> p n (t h w)", t=PACK),
+            )
+            x_grouped = grp_pool.tile([P, K_PASS * TAPS], BF16, tag="grp", align_bytes=64)
+            src = x_raw[:, 0 : PACK * CLASSES * COLS].rearrange(
+                "p (n t ph rh pw rw) -> p rh rw n ph pw t", n=IMAGES, t=PACK, ph=OUT_H, rh=2, pw=OUT_W, rw=2
+            )
+            dst = x_grouped[:, 0 : PACK * CLASSES * COLS].rearrange(
+                "p (rh rw n ph pw t) -> p rh rw n ph pw t", rh=2, rw=2, n=IMAGES, ph=OUT_H, pw=OUT_W
+            )
+            for rw in range(2):
+                nc.vector.tensor_copy(out=dst[:, 1, rw], in_=src[:, 1, rw])
+                for n in range(IMAGES):
+                    nc.scalar.copy(out=dst[:, 0, rw, n], in_=src[:, 0, rw, n])
+
+            x_codes = xq_pool.tile([P, CLASSES * COLS], U32, align_bytes=64)
+            x_scales = xq_pool.tile([P, CLASSES * COLS], U8, align_bytes=64)
+            for cls in range(CLASSES):
+                if cls == tap_class(CENTER):
+                    codes, scales = c_codes[:, g * COLS : (g + 1) * COLS], c_scales[:, g * COLS : (g + 1) * COLS]
+                else:
+                    codes, scales = x_codes[:, cls * COLS : (cls + 1) * COLS], x_scales[:, cls * COLS : (cls + 1) * COLS]
+                nc.vector.quantize_mx(
+                    out=codes.bitcast(FP8X4),
+                    scales=scales,
+                    in_=x_grouped[:, cls * PACK * COLS : (cls + 1) * PACK * COLS],
+                )
+            for tap in stream_taps:
+                cls = tap_class(tap)
+                multiply(
+                    sums[tap], tap, g, x_codes[:, cls * COLS : (cls + 1) * COLS], x_scales[:, cls * COLS : (cls + 1) * COLS]
+                )
+
+        best = keep.tile([P, IMAGES, OUT_H, OUT_W], F32)
+
+        def fold_in(tap, acc):
+            kh, kw = divmod(tap, KERNEL)
+            t = post.tile([P, IMAGES, OUT_H, OUT_W], F32)
+            r = post.tile([P, IMAGES, OUT_H, OUT_W], F32)
+            flat = "p n h w -> p (n h w)"
+            nc.scalar.activation(out=t[:].rearrange(flat), in_=acc[:], func=ACT.Identity, bias=shift_t[:])
+            nc.scalar.activation(out=r[:].rearrange(flat), in_=acc[:], func=ACT.Relu, bias=shift_r[:])
+            if tap == stream_taps[0]:
+                hs = best
+            else:
+                hs = post.tile([P, IMAGES, OUT_H, OUT_W], F32)
+            nc.vector.scalar_tensor_tensor(
+                out=hs[:].rearrange(flat), in0=r[:].rearrange(flat), scalar=6.0, in1=t[:].rearrange(flat),
+                op0=ALU.min, op1=ALU.mult,
+            )
+            if tap != stream_taps[0]:
+                dh, dw = (1 if kh == 0 else 0), (1 if kw == 0 else 0)
+                nc.vector.tensor_max(
+                    out=best[:, :, dh:OUT_H, dw:OUT_W],
+                    in0=best[:, :, dh:OUT_H, dw:OUT_W],
+                    in1=hs[:, :, 0 : OUT_H - dh, 0 : OUT_W - dw],
+                )
+
+        fold_in(stream_taps[0], sums[stream_taps[0]])
+        center_sum = acc_pool.tile([P, COLS], F32, name="acc_center", tag="acc")
+        for g in range(PASSES):
+            multiply(center_sum, CENTER, g, c_codes[:, g * COLS : (g + 1) * COLS], c_scales[:, g * COLS : (g + 1) * COLS])
+        for tap in stream_taps[1:]:
+            fold_in(tap, sums[tap])
+        fold_in(CENTER, center_sum)
+
+        flat_best = best[:].rearrange("p n h w -> p (n h w)")
+        capped = keep.tile([P, COLS], F32)
+        nc.vector.tensor_scalar_min(out=capped[:], in0=flat_best, scalar1=120.0)
+        e = keep.tile([P, COLS], F32)
+        nc.scalar.activation(out=e[:], in_=capped[:], func=ACT.Exp, scale=1.0 / 6.0)
+        u = keep.tile([P, COLS], F32)
+        nc.vector.scalar_tensor_tensor(out=u[:], in0=e[:], scalar=2.0, in1=e[:], op0=ALU.add, op1=ALU.mult)
+        inv = keep.tile([P, COLS], F32)
+        nc.vector.tensor_scalar_add(out=inv[:], in0=u[:], scalar1=2.0)
+        nc.vector.reciprocal(out=inv[:], in_=inv[:])
+        quotient = keep.tile([P, COLS], F32)
+        nc.vector.tensor_mul(out=quotient[:], in0=u[:], in1=inv[:])
+        result = keep.tile([P, COLS], F32)
+        nc.vector.scalar_tensor_tensor(
+            out=result[:], in0=flat_best, scalar=1.0 / 6.0, in1=quotient[:], op0=ALU.mult, op1=ALU.mult
+        )
+        nc.sync.dma_start(
+            out=out.rearrange("n o h w -> o n (h w)"), in_=result[:].rearrange("p (n q) -> p n q", n=IMAGES)
+        )

@@ -134,10 +134,10 @@ def tile_modelnew_pa_k_kernel(tc, x, weight, bias, out):
             )
             x_grouped = grp_pool.tile([P, K_PASS * TAPS], BF16, tag="grp", align_bytes=64)
             src = x_raw[:, 0 : PACK * CLASSES * COLS].rearrange(
-                "p (n t ph rh pw rw) -> p rh rw n ph pw t", n=IMAGES, t=PACK, ph=OUT_H, rh=2, pw=OUT_W, rw=2
+                "p (n t ph rh pw rw) -> p rh rw n ph t pw", n=IMAGES, t=PACK, ph=OUT_H, rh=2, pw=OUT_W, rw=2
             )
             dst = x_grouped[:, 0 : PACK * CLASSES * COLS].rearrange(
-                "p (rh rw n ph pw t) -> p rh rw n ph pw t", rh=2, rw=2, n=IMAGES, ph=OUT_H, pw=OUT_W
+                "p (rh rw n ph pw t) -> p rh rw n ph t pw", rh=2, rw=2, n=IMAGES, ph=OUT_H, pw=OUT_W
             )
             for rw in range(2):
                 nc.vector.tensor_copy(out=dst[:, 1, rw], in_=src[:, 1, rw])

@@ -28,8 +28,7 @@ FLOPS = 2 * TAPS * C_OUT * C_IN * COLS
 
 RAW_BUFS = 7
 GRP_BUFS = 3
-VECTOR_TAPS = 7
-REGIONS = 4
+PAIRED = 8
 
 
 def tap_class(tap):
@@ -73,12 +72,17 @@ def tile_modelnew_pa_k_kernel(tc, x, weight, bias, out):
 
                 w_sorted = sorted_pool.tile([P, K_PASS * TAPS], BF16)
                 src = w_raw[:].rearrange("o (p half e t) -> o half p e t", half=2, e=2, t=TAPS)
-                dst = w_sorted[:].rearrange("o (t half p e) -> o half p e t", half=2, e=2, t=TAPS)
+                paired = w_sorted[:, 0 : K_PASS * PAIRED].rearrange(
+                    "o (b half p t e) -> o half b p e t", half=2, p=P, t=2, e=2
+                )
                 for half in range(2):
-                    for t0 in range(0, VECTOR_TAPS, REGIONS):
-                        t1 = min(t0 + REGIONS, VECTOR_TAPS)
-                        nc.vector.tensor_copy(out=dst[:, half, :, :, t0:t1], in_=src[:, half, :, :, t0:t1])
-                    nc.scalar.copy(out=dst[:, half, :, :, VECTOR_TAPS:TAPS], in_=src[:, half, :, :, VECTOR_TAPS:TAPS])
+                    nc.vector.tensor_copy(
+                        out=paired[:, half], in_=src[:, half, :, :, 0:PAIRED].rearrange("o p e (b t) -> o b p e t", t=2)
+                    )
+                nc.scalar.copy(
+                    out=w_sorted[:, K_PASS * PAIRED : K_PASS * TAPS].rearrange("o (half p e) -> o p half e", half=2, e=2),
+                    in_=w_raw[:].rearrange("o (p half e t) -> o p half e t", half=2, e=2, t=TAPS)[:, :, :, :, PAIRED],
+                )
 
                 words = w_sorted[:].bitcast(F32)
                 w_grouped = grp_pool.tile([P, K_PASS * TAPS], BF16, tag="grp", align_bytes=64)
@@ -86,12 +90,11 @@ def tile_modelnew_pa_k_kernel(tc, x, weight, bias, out):
                 for t0 in range(0, TAPS, 2):
                     n_taps = min(2, TAPS - t0)
                     turned = turned_pool.tile([P, 2 * 2 * P], F32)
+                    pair_words = words[:, 2 * t0 * P : 2 * (t0 + n_taps) * P].rearrange(
+                        "o (half p t) -> o t half p", half=2, t=n_taps
+                    )
                     for k in range(2 * n_taps):
-                        nc.tensor.transpose(
-                            turned[:, k * P : (k + 1) * P],
-                            words[:, (2 * t0 + k) * P : (2 * t0 + k + 1) * P],
-                            ident[:],
-                        )
+                        nc.tensor.transpose(turned[:, k * P : (k + 1) * P], pair_words[:, k // 2, k % 2, :], ident[:])
                     nc.scalar.copy(
                         out=grouped_words[:, 2 * t0 * P : 2 * (t0 + n_taps) * P].rearrange(
                             "p (t o half) -> p t o half", o=P, half=2

@@ -28,7 +28,7 @@ FLOPS = 2 * TAPS * C_OUT * C_IN * COLS
 
 RAW_BUFS = 7
 GRP_BUFS = 3
-PAIRED = 8
+VECTOR_P = 104
 
 
 def tap_class(tap):
@@ -71,30 +71,20 @@ def tile_modelnew_pa_k_kernel(tc, x, weight, bias, out):
                 nc.sync.dma_start(out=w_raw[:], in_=w_rows[:, g * K_PASS * TAPS : (g + 1) * K_PASS * TAPS])
 
                 w_sorted = sorted_pool.tile([P, K_PASS * TAPS], BF16)
-                src = w_raw[:].rearrange("o (p half e t) -> o half p e t", half=2, e=2, t=TAPS)
-                paired = w_sorted[:, 0 : K_PASS * PAIRED].rearrange(
-                    "o (b half p t e) -> o half b p e t", half=2, p=P, t=2, e=2
-                )
+                src = w_raw[:].rearrange("o (p half e t) -> o p half e t", half=2, e=2, t=TAPS)
+                dst = w_sorted[:].rearrange("o (half p t e) -> o p half e t", half=2, t=TAPS, e=2)
+                nc.vector.tensor_copy(out=dst[:, 0:VECTOR_P], in_=src[:, 0:VECTOR_P])
                 for half in range(2):
-                    nc.vector.tensor_copy(
-                        out=paired[:, half], in_=src[:, half, :, :, 0:PAIRED].rearrange("o p e (b t) -> o b p e t", t=2)
-                    )
-                nc.scalar.copy(
-                    out=w_sorted[:, K_PASS * PAIRED : K_PASS * TAPS].rearrange("o (half p e) -> o p half e", half=2, e=2),
-                    in_=w_raw[:].rearrange("o (p half e t) -> o p half e t", half=2, e=2, t=TAPS)[:, :, :, :, PAIRED],
-                )
+                    nc.scalar.copy(out=dst[:, VECTOR_P:P, half], in_=src[:, VECTOR_P:P, half])
 
-                words = w_sorted[:].bitcast(F32)
+                words = w_sorted[:].bitcast(F32).rearrange("o (half p t) -> o t half p", half=2, t=TAPS)
                 w_grouped = grp_pool.tile([P, K_PASS * TAPS], BF16, tag="grp", align_bytes=64)
                 grouped_words = w_grouped[:].bitcast(F32)
                 for t0 in range(0, TAPS, 2):
                     n_taps = min(2, TAPS - t0)
                     turned = turned_pool.tile([P, 2 * 2 * P], F32)
-                    pair_words = words[:, 2 * t0 * P : 2 * (t0 + n_taps) * P].rearrange(
-                        "o (half p t) -> o t half p", half=2, t=n_taps
-                    )
                     for k in range(2 * n_taps):
-                        nc.tensor.transpose(turned[:, k * P : (k + 1) * P], pair_words[:, k // 2, k % 2, :], ident[:])
+                        nc.tensor.transpose(turned[:, k * P : (k + 1) * P], words[:, t0 + k // 2, k % 2, :], ident[:])
                     nc.scalar.copy(
                         out=grouped_words[:, 2 * t0 * P : 2 * (t0 + n_taps) * P].rearrange(
                             "p (t o half) -> p t o half", o=P, half=2

@@ -157,8 +157,7 @@ def tile_modelnew_pa_k_kernel(tc, x, weight, bias, out):
 
         best = keep.tile([P, IMAGES, OUT_H, OUT_W], F32)
 
-        def fold_in(tap, acc):
-            kh, kw = divmod(tap, KERNEL)
+        def hardswish(tap, acc):
             t = post.tile([P, IMAGES, OUT_H, OUT_W], F32)
             r = post.tile([P, IMAGES, OUT_H, OUT_W], F32)
             flat = "p n h w -> p (n h w)"
@@ -172,38 +171,56 @@ def tile_modelnew_pa_k_kernel(tc, x, weight, bias, out):
                 out=hs[:].rearrange(flat), in0=r[:].rearrange(flat), scalar=6.0, in1=t[:].rearrange(flat),
                 op0=ALU.min, op1=ALU.mult,
             )
-            if tap != stream_taps[0]:
-                dh, dw = (1 if kh == 0 else 0), (1 if kw == 0 else 0)
-                nc.vector.tensor_max(
-                    out=best[:, :, dh:OUT_H, dw:OUT_W],
-                    in0=best[:, :, dh:OUT_H, dw:OUT_W],
-                    in1=hs[:, :, 0 : OUT_H - dh, 0 : OUT_W - dw],
-                )
+            return hs
 
-        fold_in(stream_taps[0], sums[stream_taps[0]])
+        def fold_in(tap, hs):
+            kh, kw = divmod(tap, KERNEL)
+            dh, dw = (1 if kh == 0 else 0), (1 if kw == 0 else 0)
+            nc.vector.tensor_max(
+                out=best[:, :, dh:OUT_H, dw:OUT_W],
+                in0=best[:, :, dh:OUT_H, dw:OUT_W],
+                in1=hs[:, :, 0 : OUT_H - dh, 0 : OUT_W - dw],
+            )
+
+        hardswish(stream_taps[0], sums[stream_taps[0]])
         center_sum = acc_pool.tile([P, COLS], F32, name="acc_center", tag="acc")
         for g in range(PASSES):
             multiply(center_sum, CENTER, g, c_codes[:, g * COLS : (g + 1) * COLS], c_scales[:, g * COLS : (g + 1) * COLS])
-        for tap in stream_taps[1:]:
-            fold_in(tap, sums[tap])
-        fold_in(CENTER, center_sum)
+        sums[CENTER] = center_sum
+        waiting = []
+        for tap in stream_taps[1:] + [CENTER]:
+            waiting.append((tap, hardswish(tap, sums[tap])))
+            if len(waiting) == 2:
+                fold_in(waiting[0][0], waiting[0][1])
+                waiting.remove(waiting[0])
+        fold_in(waiting[0][0], waiting[0][1])
 
         flat_best = best[:].rearrange("p n h w -> p (n h w)")
         capped = keep.tile([P, COLS], F32)
-        nc.vector.tensor_scalar_min(out=capped[:], in0=flat_best, scalar1=120.0)
         e = keep.tile([P, COLS], F32)
-        nc.scalar.activation(out=e[:], in_=capped[:], func=ACT.Exp, scale=1.0 / 6.0)
         u = keep.tile([P, COLS], F32)
-        nc.vector.scalar_tensor_tensor(out=u[:], in0=e[:], scalar=2.0, in1=e[:], op0=ALU.add, op1=ALU.mult)
         inv = keep.tile([P, COLS], F32)
-        nc.vector.tensor_scalar_add(out=inv[:], in0=u[:], scalar1=2.0)
-        nc.vector.reciprocal(out=inv[:], in_=inv[:])
         quotient = keep.tile([P, COLS], F32)
-        nc.vector.tensor_mul(out=quotient[:], in0=u[:], in1=inv[:])
         result = keep.tile([P, COLS], F32)
-        nc.vector.scalar_tensor_tensor(
-            out=result[:], in0=flat_best, scalar=1.0 / 6.0, in1=quotient[:], op0=ALU.mult, op1=ALU.mult
-        )
-        nc.sync.dma_start(
-            out=out.rearrange("n o h w -> o n (h w)"), in_=result[:].rearrange("p (n q) -> p n q", n=IMAGES)
-        )
+        halves = [slice(k * COLS // 2, (k + 1) * COLS // 2) for k in range(2)]
+        for s in halves:
+            nc.vector.tensor_scalar_min(out=capped[:, s], in0=flat_best[:, s], scalar1=120.0)
+        for s in halves:
+            nc.scalar.activation(out=e[:, s], in_=capped[:, s], func=ACT.Exp, scale=1.0 / 6.0)
+        for s in halves:
+            nc.vector.scalar_tensor_tensor(out=u[:, s], in0=e[:, s], scalar=2.0, in1=e[:, s], op0=ALU.add, op1=ALU.mult)
+        for s in halves:
+            nc.vector.tensor_scalar_add(out=inv[:, s], in0=u[:, s], scalar1=2.0)
+        for s in halves:
+            nc.vector.reciprocal(out=inv[:, s], in_=inv[:, s])
+        for s in halves:
+            nc.vector.tensor_mul(out=quotient[:, s], in0=u[:, s], in1=inv[:, s])
+        for k in range(2):
+            s = halves[k]
+            nc.vector.scalar_tensor_tensor(
+                out=result[:, s], in0=flat_best[:, s], scalar=1.0 / 6.0, in1=quotient[:, s], op0=ALU.mult, op1=ALU.mult
+            )
+            nc.sync.dma_start(
+                out=out[k * IMAGES // 2 : (k + 1) * IMAGES // 2].rearrange("n o h w -> o n (h w)"),
+                in_=result[:, s].rearrange("p (n q) -> p n q", n=IMAGES // 2),
+            )

from contextlib import ExitStack

import concourse.mybir as mybir
from concourse.masks import make_identity

BF16 = mybir.dt.bfloat16
F32 = mybir.dt.float32
U32 = mybir.dt.uint32
U8 = mybir.dt.uint8
FP8X4 = mybir.dt.float8_e4m3fn_x4
ACT = mybir.ActivationFunctionType
ALU = mybir.AluOpType

P = 128
PACK = 4
K_PASS = P * PACK
IMAGES, C_IN, HEIGHT, WIDTH = 4, 8192, 16, 16
C_OUT, KERNEL = 128, 3
TAPS = KERNEL * KERNEL
PASSES = C_IN // K_PASS
OUT_H, OUT_W = HEIGHT // 2, WIDTH // 2
COLS = IMAGES * OUT_H * OUT_W
CLASSES = 4
W_COLS = TAPS * C_OUT
CENTER = 4

FLOPS = 2 * TAPS * C_OUT * C_IN * COLS

RAW_BUFS = 7
GRP_BUFS = 3
VECTOR_P = 104


def tap_class(tap):
    kh, kw = divmod(tap, KERNEL)
    return 2 * ((kh - 1) % 2) + (kw - 1) % 2


def tile_modelnew_pa_k_kernel(tc, x, weight, bias, out):
    nc = tc.nc
    with ExitStack() as stack:
        keep = stack.enter_context(tc.tile_pool(name="keep", bufs=1))
        raw_pool = stack.enter_context(tc.tile_pool(name="raw", bufs=RAW_BUFS))
        grp_pool = stack.enter_context(tc.tile_pool(name="grp", bufs=GRP_BUFS))

        ident = keep.tile([P, P], F32)
        make_identity(nc, ident[:])

        zero = keep.tile([P, 1], F32)
        one = keep.tile([P, 1], F32)
        nc.vector.memset(zero[:], 0.0)
        nc.scalar.activation(out=one[:], in_=zero[:], func=ACT.Exp)

        bias_bf = keep.tile([P, 1], BF16)
        with nc.allow_non_contiguous_dma(reason="128 bias values, one to a partition"):
            nc.sync.dma_start(out=bias_bf[:], in_=bias.rearrange("(o one) -> o one", one=1))
        shift_t = keep.tile([P, 1], F32)
        shift_r = keep.tile([P, 1], F32)
        nc.vector.tensor_scalar_add(out=shift_t[:], in0=bias_bf[:], scalar1=-0.5)
        nc.vector.tensor_scalar_add(out=shift_r[:], in0=bias_bf[:], scalar1=2.5)

        w_codes = keep.tile([P, PASSES * W_COLS], U32, align_bytes=64)
        w_scales = keep.tile([P, PASSES * W_COLS], U8, align_bytes=64)
        c_codes = keep.tile([P, PASSES * COLS], U32, align_bytes=64)
        c_scales = keep.tile([P, PASSES * COLS], U8, align_bytes=64)

        w_rows = weight.rearrange("o c kh kw -> o (c kh kw)")
        with tc.tile_pool(name="sorted", bufs=2) as sorted_pool, tc.psum_pool(name="turned", bufs=8) as turned_pool:
            for g in range(PASSES):
                w_raw = raw_pool.tile([P, K_PASS * TAPS], BF16, tag="raw")
                nc.sync.dma_start(out=w_raw[:], in_=w_rows[:, g * K_PASS * TAPS : (g + 1) * K_PASS * TAPS])

                w_sorted = sorted_pool.tile([P, K_PASS * TAPS], BF16)
                src = w_raw[:].rearrange("o (p half e t) -> o p half e t", half=2, e=2, t=TAPS)
                dst = w_sorted[:].rearrange("o (half p t e) -> o p half e t", half=2, t=TAPS, e=2)
                nc.vector.tensor_copy(out=dst[:, 0:VECTOR_P], in_=src[:, 0:VECTOR_P])
                for half in range(2):
                    nc.scalar.copy(out=dst[:, VECTOR_P:P, half], in_=src[:, VECTOR_P:P, half])

                words = w_sorted[:].bitcast(F32).rearrange("o (half p t) -> o t half p", half=2, t=TAPS)
                w_grouped = grp_pool.tile([P, K_PASS * TAPS], BF16, tag="grp", align_bytes=64)
                grouped_words = w_grouped[:].bitcast(F32)
                for t0 in range(0, TAPS, 2):
                    n_taps = min(2, TAPS - t0)
                    turned = turned_pool.tile([P, 2 * 2 * P], F32)
                    for k in range(2 * n_taps):
                        nc.tensor.transpose(turned[:, k * P : (k + 1) * P], words[:, t0 + k // 2, k % 2, :], ident[:])
                    nc.scalar.copy(
                        out=grouped_words[:, 2 * t0 * P : 2 * (t0 + n_taps) * P].rearrange(
                            "p (t o half) -> p t o half", o=P, half=2
                        ),
                        in_=turned[:, 0 : 2 * n_taps * P].rearrange("p (t half o) -> p t o half", o=P, half=2),
                    )

                for c0, c1 in ((0, 1024), (1024, W_COLS)):
                    nc.vector.quantize_mx(
                        out=w_codes[:, g * W_COLS + c0 : g * W_COLS + c1].bitcast(FP8X4),
                        scales=w_scales[:, g * W_COLS + c0 : g * W_COLS + c1],
                        in_=w_grouped[:, PACK * c0 : PACK * c1],
                    )

        xq_pool = stack.enter_context(tc.tile_pool(name="xq", bufs=3))
        post = stack.enter_context(tc.tile_pool(name="post", bufs=2))
        acc_pool = stack.enter_context(tc.psum_pool(name="acc", bufs=8))

        def multiply(acc, tap, g, codes, scales):
            nc.tensor.matmul_mx(
                out=acc[:],
                lhsT=w_codes[:, g * W_COLS + tap * C_OUT : g * W_COLS + (tap + 1) * C_OUT].bitcast(FP8X4),
                lhsT_scale=w_scales[:, g * W_COLS + tap * C_OUT : g * W_COLS + (tap + 1) * C_OUT],
                rhs=codes.bitcast(FP8X4),
                rhs_scale=scales,
                start=(g == 0),
                stop=(g == PASSES - 1),
            )

        stream_taps = [tap for tap in reversed(range(TAPS)) if tap != CENTER]
        sums = {}
        for tap in stream_taps:
            sums[tap] = acc_pool.tile([P, COLS], F32, name="acc%d" % tap, tag="acc")

        for g in range(PASSES):
            x_raw = raw_pool.tile([P, K_PASS * TAPS], BF16, tag="raw")
            nc.sync.dma_start(
                out=x_raw[:, 0 : PACK * CLASSES * COLS].rearrange("p (n q) -> p n q", n=IMAGES),
                in_=x[:, g * K_PASS : (g + 1) * K_PASS, :, :].rearrange("n (p t) h w -> p n (t h w)", t=PACK),
            )
            x_grouped = grp_pool.tile([P, K_PASS * TAPS], BF16, tag="grp", align_bytes=64)
            src = x_raw[:, 0 : PACK * CLASSES * COLS].rearrange(
                "p (n t ph rh pw rw) -> p rh rw n ph t pw", n=IMAGES, t=PACK, ph=OUT_H, rh=2, pw=OUT_W, rw=2
            )
            dst = x_grouped[:, 0 : PACK * CLASSES * COLS].rearrange(
                "p (rh rw n ph pw t) -> p rh rw n ph t pw", rh=2, rw=2, n=IMAGES, ph=OUT_H, pw=OUT_W
            )
            for rw in range(2):
                nc.vector.tensor_copy(out=dst[:, 1, rw], in_=src[:, 1, rw])
                for n in range(IMAGES):
                    nc.scalar.copy(out=dst[:, 0, rw, n], in_=src[:, 0, rw, n])

            x_codes = xq_pool.tile([P, CLASSES * COLS], U32, align_bytes=64)
            x_scales = xq_pool.tile([P, CLASSES * COLS], U8, align_bytes=64)
            for cls in range(CLASSES):
                if cls == tap_class(CENTER):
                    codes, scales = c_codes[:, g * COLS : (g + 1) * COLS], c_scales[:, g * COLS : (g + 1) * COLS]
                else:
                    codes, scales = x_codes[:, cls * COLS : (cls + 1) * COLS], x_scales[:, cls * COLS : (cls + 1) * COLS]
                nc.vector.quantize_mx(
                    out=codes.bitcast(FP8X4),
                    scales=scales,
                    in_=x_grouped[:, cls * PACK * COLS : (cls + 1) * PACK * COLS],
                )
            for tap in stream_taps:
                cls = tap_class(tap)
                multiply(
                    sums[tap], tap, g, x_codes[:, cls * COLS : (cls + 1) * COLS], x_scales[:, cls * COLS : (cls + 1) * COLS]
                )

        best = keep.tile([P, IMAGES, OUT_H, OUT_W], F32)

        def hardswish(tap, acc):
            t = post.tile([P, IMAGES, OUT_H, OUT_W], F32)
            r = post.tile([P, IMAGES, OUT_H, OUT_W], F32)
            flat = "p n h w -> p (n h w)"
            nc.scalar.activation(out=t[:].rearrange(flat), in_=acc[:], func=ACT.Identity, bias=shift_t[:])
            nc.scalar.activation(out=r[:].rearrange(flat), in_=acc[:], func=ACT.Relu, bias=shift_r[:])
            if tap == stream_taps[0]:
                hs = best
            else:
                hs = post.tile([P, IMAGES, OUT_H, OUT_W], F32)
            nc.vector.scalar_tensor_tensor(
                out=hs[:].rearrange(flat), in0=r[:].rearrange(flat), scalar=6.0, in1=t[:].rearrange(flat),
                op0=ALU.min, op1=ALU.mult,
            )
            return hs

        def fold_in(tap, hs):
            kh, kw = divmod(tap, KERNEL)
            dh, dw = (1 if kh == 0 else 0), (1 if kw == 0 else 0)
            nc.vector.tensor_max(
                out=best[:, :, dh:OUT_H, dw:OUT_W],
                in0=best[:, :, dh:OUT_H, dw:OUT_W],
                in1=hs[:, :, 0 : OUT_H - dh, 0 : OUT_W - dw],
            )

        hardswish(stream_taps[0], sums[stream_taps[0]])
        center_sum = acc_pool.tile([P, COLS], F32, name="acc_center", tag="acc")
        for g in range(PASSES):
            multiply(center_sum, CENTER, g, c_codes[:, g * COLS : (g + 1) * COLS], c_scales[:, g * COLS : (g + 1) * COLS])
        sums[CENTER] = center_sum
        waiting = []
        for tap in stream_taps[1:] + [CENTER]:
            waiting.append((tap, hardswish(tap, sums[tap])))
            if len(waiting) == 2:
                fold_in(waiting[0][0], waiting[0][1])
                waiting.remove(waiting[0])
        fold_in(waiting[0][0], waiting[0][1])

        flat_best = best[:].rearrange("p n h w -> p (n h w)")
        capped = keep.tile([P, COLS], F32)
        e = keep.tile([P, COLS], F32)
        u = keep.tile([P, COLS], F32)
        inv = keep.tile([P, COLS], F32)
        quotient = keep.tile([P, COLS], F32)
        result = keep.tile([P, COLS], F32)
        halves = [slice(k * COLS // 2, (k + 1) * COLS // 2) for k in range(2)]
        for s in halves:
            nc.vector.tensor_scalar_min(out=capped[:, s], in0=flat_best[:, s], scalar1=120.0)
        for s in halves:
            nc.scalar.activation(out=e[:, s], in_=capped[:, s], func=ACT.Exp, scale=1.0 / 6.0)
        for s in halves:
            nc.vector.scalar_tensor_tensor(out=u[:, s], in0=e[:, s], scalar=2.0, in1=e[:, s], op0=ALU.add, op1=ALU.mult)
        for s in halves:
            nc.vector.tensor_scalar_add(out=inv[:, s], in0=u[:, s], scalar1=2.0)
        for s in halves:
            nc.vector.reciprocal(out=inv[:, s], in_=inv[:, s])
        for s in halves:
            nc.vector.tensor_mul(out=quotient[:, s], in0=u[:, s], in1=inv[:, s])
        for k in range(2):
            s = halves[k]
            nc.vector.scalar_tensor_tensor(
                out=result[:, s], in0=flat_best[:, s], scalar=1.0 / 6.0, in1=quotient[:, s], op0=ALU.mult, op1=ALU.mult
            )
            nc.sync.dma_start(
                out=out[k * IMAGES // 2 : (k + 1) * IMAGES // 2].rearrange("n o h w -> o n (h w)"),
                in_=result[:, s].rearrange("p (n q) -> p n q", n=IMAGES // 2),
            )
